import numpy as np
import ml_dtypes


def mxq(x, axis, fmt="e4m3"):
    dtype, down = {"e4m3": (ml_dtypes.float8_e4m3fn, 7), "e5m2": (ml_dtypes.float8_e5m2, 14)}[fmt]
    v = np.moveaxis(np.asarray(x, np.float32).astype(ml_dtypes.bfloat16).astype(np.float64), axis, -1)
    blocks = v.reshape(v.shape[:-1] + (-1, 32))
    amax = np.abs(blocks).max(-1, keepdims=True)
    byte = np.maximum(np.where(amax > 0, np.frexp(amax)[1] - 1 + 127, 0) - down, 1)
    scale = np.exp2(byte - 127.0)
    codes = (blocks / scale).astype(np.float32).astype(dtype).astype(np.float64)
    return np.moveaxis((codes * scale).reshape(v.shape), -1, axis)


WIDE = False


def mx_kscale(k):
    if not WIDE:
        return np.ones(k)
    levels = np.array([10, -10, 5, -5, 0])
    a = np.random.permutation(np.resize(levels, k // 512 * 4)).reshape(k // 512, 4)
    idx = np.arange(k)
    return np.exp2(a[idx // 512, idx % 128 // 32])


BF16 = ml_dtypes.bfloat16


def bf(x):
    return np.asarray(x, np.float32).astype(BF16)


def f64(x):
    return np.asarray(x).astype(np.float64)


E2M1 = np.array([0.0, 0.5, 1.0, 1.5, 2.0, 3.0, 4.0, 6.0, -0.0, -0.5, -1.0, -1.5, -2.0, -3.0, -4.0, -6.0])


def pack_weight(w, fmt):
    k, n = w.shape
    w = f64(bf(w)).reshape(k // 32, 32, n)
    amax = np.abs(w).max(1)
    if fmt == "e4m3":
        byte = np.frexp(amax)[1] - 1 + 127 - 7
    else:
        mant, ex = np.frexp(amax / 6.0)
        byte = np.where(mant > 0.5, ex, ex - 1) + 127
    byte = np.clip(np.where(amax > 0, byte, 1), 1, 254)
    scaled = (w * np.exp2(127.0 - byte)[:, None, :]).reshape(k, n).astype(np.float32)
    by_word = np.ascontiguousarray(scaled.reshape(k // 512, 128, 4, n).transpose(0, 1, 3, 2))
    if fmt == "e4m3":
        words = by_word.astype(ml_dtypes.float8_e4m3fn).view(np.uint8)
    else:
        c = by_word.astype(ml_dtypes.float4_e2m1fn).view(np.uint8) & 0xF
        words = c[..., 0::2] | (c[..., 1::2] << 4)
    return np.ascontiguousarray(words), np.ascontiguousarray(byte.astype(np.uint8).reshape(k // 512, 16, n))


def unpack_weight(words, scales, fmt):
    g, p, n, _ = words.shape
    if fmt == "e4m3":
        vals = np.ascontiguousarray(words).view(ml_dtypes.float8_e4m3fn).astype(np.float64)
    else:
        nib = np.empty((g, p, n, 4), np.uint8)
        nib[..., 0::2] = words & 0xF
        nib[..., 1::2] = words >> 4
        vals = E2M1[nib]
    vals = vals * np.repeat(np.exp2(scales.astype(np.float64) - 127.0), 8, axis=1)[..., None]
    return vals.transpose(0, 1, 3, 2).reshape(g * 512, n)


B, IN_F, FEAT, NCLASS = 4096, 512, 128, 256
D = 4 * FEAT
GAMMA = 0.1
FMT = "e4m3"


def setup_inputs():
    s = mx_kscale(IN_F)
    ws = 0.5 / np.sqrt(IN_F)
    x = bf(np.random.standard_normal((B, IN_F)) * s)
    x_90 = bf(np.random.standard_normal((B, IN_F)) * s)
    x_180 = bf(np.random.standard_normal((B, IN_F)) * s)
    x_270 = bf(np.random.standard_normal((B, IN_F)) * s)
    wf_words, wf_scales = pack_weight((np.random.standard_normal((FEAT, IN_F)) * ws / s).T, FMT)
    b_f = bf(np.random.standard_normal(FEAT) * 0.25)
    wr_words, wr_scales = pack_weight((np.random.standard_normal((FEAT, IN_F)) * ws / s).T, FMT)
    b_r = bf(np.random.standard_normal(FEAT) * 0.25)
    centers = bf(0.2 + 0.3 * np.random.standard_normal((NCLASS, D)))
    return {
        "x": x,
        "x_90": x_90,
        "x_180": x_180,
        "x_270": x_270,
        "W_f_words": wf_words,
        "W_f_scales": wf_scales,
        "b_f": b_f,
        "W_r_words": wr_words,
        "W_r_scales": wr_scales,
        "b_r": b_r,
        "centers": centers,
    }


def reference(x, x_90, x_180, x_270, W_f_words, W_f_scales, b_f, W_r_words, W_r_scales, b_r, centers):
    wf = unpack_weight(W_f_words, W_f_scales, FMT).T
    wr = unpack_weight(W_r_words, W_r_scales, FMT).T
    f = np.maximum((mxq(f64(x), 1, "e4m3") @ wf.T) + f64(b_f), 0.0)
    f90 = np.maximum((mxq(f64(x_90), 1, "e4m3") @ wr.T) + f64(b_r), 0.0)
    f180 = np.maximum((mxq(f64(x_180), 1, "e4m3") @ wr.T) + f64(b_r), 0.0)
    f270 = np.maximum((mxq(f64(x_270), 1, "e4m3") @ wr.T) + f64(b_r), 0.0)
    feat = np.concatenate((f, f90, f180, f270), axis=1)
    c = f64(centers)
    f2 = np.sum(feat * feat, axis=1, keepdims=True)
    c2 = np.sum(c * c, axis=1)
    d2 = f2 + c2[None, :] - 2.0 * (mxq(feat, 1, "e4m3") @ mxq(c, 1, "e4m3").T)
    return np.sqrt(np.maximum(d2, 0.0)) * (-GAMMA)

@@ -1,0 +1,285 @@
+from contextlib import ExitStack
+
+import concourse.masks as masks
+import concourse.mybir as mybir
+
+F32 = mybir.dt.float32
+BF16 = mybir.dt.bfloat16
+U8 = mybir.dt.uint8
+U32 = mybir.dt.uint32
+I32 = mybir.dt.int32
+FP8X4 = mybir.dt.float8_e4m3fn_x4
+ACT = mybir.ActivationFunctionType
+ALU = mybir.AluOpType
+
+P = 128
+PACK = 4
+BATCH = 4096
+IN_F = 512
+FEAT = 128
+VIEWS = 4
+NCLASS = 256
+GAMMA = 0.1
+
+CHUNK = 512
+SLOTS = CHUNK // P
+CHUNKS = BATCH // CHUNK
+UNITS = 2 * CHUNKS
+
+FLOPS = 2 * BATCH * IN_F * FEAT * VIEWS + 2 * BATCH * FEAT * VIEWS * NCLASS
+
+AT_PROJECT = 1
+AT_RELU = 2
+AT_SQUARES = 4
+AT_SCORE = 5
+AT_DISTANCE = 6
+AT_ROOT = 7
+AT_STORE = 8
+
+
+def tile_qccpn_pa_t_kernel(
+    tc, x, x_90, x_180, x_270, W_f_words, W_f_scales, b_f, W_r_words, W_r_scales, b_r, centers, out
+):
+    nc = tc.nc
+    views = (x, x_90, x_180, x_270)
+    weight_of_view = (0, 1, 1, 1)
+
+    with ExitStack() as ctx:
+        const = ctx.enter_context(tc.tile_pool(name="const", bufs=1))
+        x_pool = ctx.enter_context(tc.tile_pool(name="x", bufs=1))
+        work = ctx.enter_context(tc.tile_pool(name="work", bufs=2))
+        psum = ctx.enter_context(tc.psum_pool(name="psum", bufs=1))
+
+        ident_f32 = const.tile([P, P], F32)
+        masks.make_identity(nc, ident_f32[:])
+        ident_bf16 = const.tile([P, P], BF16)
+        masks.make_identity(nc, ident_bf16[:])
+
+        w_codes = const.tile([P, 2, FEAT], U32, align_bytes=64)
+        w_scales = const.tile([P, 2, FEAT], U8, align_bytes=64)
+        nc.vector.memset(w_scales[:].rearrange("p w n -> p (w n)").bitcast(I32), 0)
+        bias_rows = const.tile([P, P], BF16)
+        nc.vector.memset(bias_rows[:], 0.0)
+
+        centres_in = const.tile([P, 2, VIEWS * FEAT], BF16)
+        x_sb = {}
+
+        def load_view(c, v):
+            x_sb[(c, v)] = x_pool.tile([P, SLOTS, IN_F], BF16, name="x_%d_%d" % (c, v))
+            rows = views[v][c * CHUNK : (c + 1) * CHUNK, :]
+            nc.sync.dma_start(out=x_sb[(c, v)][:], in_=rows.rearrange("(r s) k -> r s k", s=SLOTS))
+
+        def load_weight(w, words, scales):
+            for quadrant in range(4):
+                nc.sync.dma_start(
+                    out=w_scales[32 * quadrant : 32 * quadrant + 4, w, :].bitcast(I32),
+                    in_=scales[0, 4 * quadrant : 4 * quadrant + 4, :].bitcast(I32),
+                )
+            nc.sync.dma_start(
+                out=w_codes[:, w, :].bitcast(I32),
+                in_=words[0].rearrange("p n t -> p (n t)").bitcast(I32),
+            )
+
+        nc.scalar.dma_start(out=bias_rows[0:1, :], in_=b_f.rearrange("(o n) -> o n", o=1))
+        nc.scalar.dma_start(out=bias_rows[1:2, :], in_=b_r.rearrange("(o n) -> o n", o=1))
+        nc.sync.dma_start(out=centres_in[:], in_=centers.rearrange("(h c) j -> c h j", c=P))
+        load_view(0, 0)
+        load_view(0, 1)
+        load_weight(0, W_f_words, W_f_scales)
+        load_weight(1, W_r_words, W_r_scales)
+        load_view(0, 2)
+        load_view(0, 3)
+        for c in range(1, CHUNKS):
+            for v in range(VIEWS):
+                load_view(c, v)
+
+        bias_t = psum.tile([P, P], BF16, tag="ft")
+        nc.tensor.transpose(out=bias_t[:], in_=bias_rows[:], identity=ident_bf16[:])
+        bias = const.tile([P, 2], F32)
+        nc.vector.tensor_copy(out=bias[:], in_=bias_t[:, 0:2])
+
+        centres_t = psum.tile([P, 2, VIEWS, P], BF16, tag="z", bufs=2)
+        for h in range(2):
+            for t in range(VIEWS):
+                nc.tensor.transpose(
+                    out=centres_t[:, h, t, :], in_=centres_in[:, h, t * FEAT : (t + 1) * FEAT], identity=ident_bf16[:]
+                )
+        centres_grouped = const.tile([P, 2, P, PACK], BF16, align_bytes=64)
+        nc.vector.tensor_copy(out=centres_grouped[:], in_=centres_t[:].rearrange("p h t c -> p h c t"))
+        c_codes = const.tile([P, NCLASS], U32, align_bytes=64)
+        c_scales = const.tile([P, NCLASS], U8, align_bytes=64)
+        nc.vector.quantize_mx(
+            out=c_codes[:].bitcast(FP8X4),
+            scales=c_scales[:],
+            in_=centres_grouped[:].rearrange("p h c t -> p (h c t)"),
+        )
+
+        c2_column = const.tile([P, 2], F32)
+        c2_repeated = const.tile([P, 2, P], F32)
+        c2_t = psum.tile([P, 2, P], F32, tag="g")
+        for h in range(2):
+            unread = work.tile([P, VIEWS * FEAT], BF16, tag="unread", bufs=4)
+            nc.scalar.activation(
+                out=unread[:], in_=centres_in[:, h, :], func=ACT.Square, accum_out=c2_column[:, h : h + 1]
+            )
+            nc.vector.tensor_copy(out=c2_repeated[:, h, :], in_=c2_column[:, h : h + 1].to_broadcast([P, P]))
+            nc.tensor.transpose(out=c2_t[:, h, :], in_=c2_repeated[:, h, :], identity=ident_f32[:])
+        c2_twice = const.tile([P, 2, NCLASS], F32)
+        for j in range(2):
+            nc.vector.tensor_copy(out=c2_twice[:, j, :], in_=c2_t[:].rearrange("p h c -> p (h c)"))
+
+        grouped = {}
+        x_codes = {}
+        x_scales = {}
+        z_bank = {}
+        feat = {}
+        f_grouped = {}
+        f_codes = {}
+        f_scales = {}
+        f2 = {}
+        g_bank = {}
+        dist = {}
+
+        def live(u):
+            return 0 <= u < UNITS
+
+        def transpose_view(u, j):
+            x_rows = x_sb[(u // 2, 2 * (u % 2) + j)]
+            grouped[(u, j)] = work.tile([P, SLOTS, P, PACK], BF16, tag="grouped", bufs=4, align_bytes=64, name="grouped")
+            for half in range(2):
+                xt = psum.tile([P, 2, 2, P], F32, tag="xt", bufs=4)
+                for i in range(2):
+                    words = x_rows[:, 2 * half + i, :].bitcast(F32)
+                    for e in range(2):
+                        nc.tensor.transpose(out=xt[:, i, e, :], in_=words[:, e : IN_F // 2 : 2], identity=ident_f32[:])
+                target = grouped[(u, j)][:, 2 * half : 2 * half + 2, :, :].bitcast(F32)
+                source = xt[:].rearrange("p i e r -> p i r e")
+                if half == 0:
+                    nc.scalar.copy(out=target, in_=source)
+                else:
+                    nc.vector.tensor_copy(out=target, in_=source)
+
+        def quantise_view(u, j):
+            x_codes[(u, j)] = work.tile([P, CHUNK], U32, tag="x_codes", bufs=4, align_bytes=64, name="x_codes")
+            x_scales[(u, j)] = work.tile([P, CHUNK], U8, tag="x_scales", bufs=4, align_bytes=64, name="x_scales")
+            nc.vector.quantize_mx(
+                out=x_codes[(u, j)][:].bitcast(FP8X4),
+                scales=x_scales[(u, j)][:],
+                in_=grouped[(u, j)][:].rearrange("p s r t -> p (s r t)"),
+            )
+
+        def project_view(u, j):
+            w = weight_of_view[2 * (u % 2) + j]
+            z_bank[(u, j)] = psum.tile([P, CHUNK], F32, tag="z", bufs=2, name="z")
+            nc.tensor.matmul_mx(
+                out=z_bank[(u, j)][:],
+                lhsT=w_codes[:, w, :].bitcast(FP8X4),
+                lhsT_scale=w_scales[:, w, :],
+                rhs=x_codes[(u, j)][:].bitcast(FP8X4),
+                rhs_scale=x_scales[(u, j)][:],
+                start=True,
+                stop=True,
+            )
+
+        def relu_view(u, j):
+            c = u // 2
+            v = 2 * (u % 2) + j
+            w = weight_of_view[v]
+            if v == 0:
+                feat[c] = work.tile([P, VIEWS, CHUNK], F32, tag="feat", bufs=2, name="feat")
+            nc.scalar.activation(
+                out=feat[c][:, v, :], in_=z_bank[(u, j)][:], func=ACT.Relu, bias=bias[:, w : w + 1], scale=1.0
+            )
+
+        def square_sum(u, j):
+            slot = 2 * (u % 2) + j
+            if j == 0:
+                f2[u] = work.tile([P, 2], F32, tag="f2", bufs=4, name="f2")
+            ft = psum.tile([P, VIEWS, FEAT], F32, tag="ft")
+            for v in range(VIEWS):
+                nc.tensor.transpose(
+                    out=ft[:, v, :], in_=feat[u // 2][:, v, slot * P : (slot + 1) * P], identity=ident_f32[:]
+                )
+            unread = work.tile([P, VIEWS * FEAT], BF16, tag="unread", bufs=4)
+            nc.scalar.activation(
+                out=unread[:], in_=ft[:].rearrange("p v f -> p (v f)"), func=ACT.Square, accum_out=f2[u][:, j : j + 1]
+            )
+
+        def regroup_features(u):
+            columns = slice(2 * (u % 2) * P, (2 * (u % 2) + 2) * P)
+            f_grouped[u] = work.tile([P, 2 * P, PACK], BF16, tag="f_grouped", bufs=3, align_bytes=64, name="f_grouped")
+            nc.vector.tensor_copy(out=f_grouped[u][:], in_=feat[u // 2][:, :, columns].rearrange("p v n -> p n v"))
+
+        def quantise_features(u):
+            f_codes[u] = work.tile([P, 2 * P], U32, tag="f_codes", bufs=2, align_bytes=64, name="f_codes")
+            f_scales[u] = work.tile([P, 2 * P], U8, tag="f_scales", bufs=2, align_bytes=64, name="f_scales")
+            nc.vector.quantize_mx(
+                out=f_codes[u][:].bitcast(FP8X4),
+                scales=f_scales[u][:],
+                in_=f_grouped[u][:].rearrange("p n v -> p (n v)"),
+            )
+
+        def score(u):
+            g_bank[u] = psum.tile([P, 2, NCLASS], F32, tag="g", name="g")
+            for j in range(2):
+                nc.tensor.matmul_mx(
+                    out=g_bank[u][:, j, :],
+                    lhsT=f_codes[u][:, j * P : (j + 1) * P].bitcast(FP8X4),
+                    lhsT_scale=f_scales[u][:, j * P : (j + 1) * P],
+                    rhs=c_codes[:].bitcast(FP8X4),
+                    rhs_scale=c_scales[:],
+                    start=True,
+                    stop=True,
+                )
+
+        def squared_distance(u):
+            dist[u] = work.tile([P, 2, NCLASS], F32, tag="dist", bufs=6, name="dist")
+            nc.vector.scalar_tensor_tensor(
+                out=dist[u][:], in0=g_bank[u][:], scalar=-2.0, in1=c2_twice[:], op0=ALU.mult, op1=ALU.add
+            )
+            for j in range(2):
+                nc.vector.tensor_scalar(
+                    out=dist[u][:, j, :],
+                    in0=dist[u][:, j, :],
+                    scalar1=f2[u][:, j : j + 1],
+                    scalar2=0.0,
+                    op0=ALU.add,
+                    op1=ALU.max,
+                )
+
+        def root(u):
+            nc.scalar.activation(out=dist[u][:], in_=dist[u][:], func=ACT.Sqrt)
+
+        def scale_and_store(u):
+            nc.vector.tensor_scalar(out=dist[u][:], in0=dist[u][:], scalar1=-GAMMA, scalar2=None, op0=ALU.mult)
+            c = u // 2
+            rows = out[c * CHUNK : (c + 1) * CHUNK, :].rearrange("(r s) n -> r s n", s=SLOTS)
+            nc.sync.dma_start(out=rows[:, 2 * (u % 2) : 2 * (u % 2) + 2, :], in_=dist[u][:])
+
+        with tc.manual_schedule():
+            for step in range(UNITS + AT_STORE):
+                for j in range(2):
+                    if live(step - AT_PROJECT):
+                        quantise_view(step - AT_PROJECT, j)
+                if live(step - AT_SCORE):
+                    quantise_features(step - AT_SCORE)
+                if live(step - AT_DISTANCE):
+                    squared_distance(step - AT_DISTANCE)
+                for j in range(2):
+                    if live(step - AT_SQUARES):
+                        square_sum(step - AT_SQUARES, j)
+                    if live(step - AT_RELU):
+                        relu_view(step - AT_RELU, j)
+                    if live(step):
+                        transpose_view(step, j)
+                if live(step - AT_SQUARES):
+                    regroup_features(step - AT_SQUARES)
+                for j in range(2):
+                    if live(step - AT_PROJECT):
+                        project_view(step - AT_PROJECT, j)
+                if live(step - AT_SCORE):
+                    score(step - AT_SCORE)
+                if live(step - AT_ROOT):
+                    root(step - AT_ROOT)
+                if live(step - AT_STORE):
+                    scale_and_store(step - AT_STORE)

@@ -48,7 +48,7 @@ def tile_qccpn_pa_t_kernel(
         const = ctx.enter_context(tc.tile_pool(name="const", bufs=1))
         x_pool = ctx.enter_context(tc.tile_pool(name="x", bufs=1))
         work = ctx.enter_context(tc.tile_pool(name="work", bufs=2))
-        psum = ctx.enter_context(tc.psum_pool(name="psum", bufs=1))
+        psum = ctx.enter_context(tc.psum_pool(name="psum", bufs=8))
 
         ident_f32 = const.tile([P, P], F32)
         masks.make_identity(nc, ident_f32[:])
@@ -60,6 +60,10 @@ def tile_qccpn_pa_t_kernel(
         nc.vector.memset(w_scales[:].rearrange("p w n -> p (w n)").bitcast(I32), 0)
         bias_rows = const.tile([P, P], BF16)
         nc.vector.memset(bias_rows[:], 0.0)
+
+        one = const.tile([P, 1], F32)
+        nc.vector.memset(one[:], 1.0)
+        nc.scalar.activation(out=one[:], in_=one[:], func=ACT.Sqrt)
 
         centres_in = const.tile([P, 2, VIEWS * FEAT], BF16)
         x_sb = {}
@@ -93,12 +97,12 @@ def tile_qccpn_pa_t_kernel(
             for v in range(VIEWS):
                 load_view(c, v)
 
-        bias_t = psum.tile([P, P], BF16, tag="ft")
+        bias_t = psum.tile([P, P], BF16, tag="bank")
         nc.tensor.transpose(out=bias_t[:], in_=bias_rows[:], identity=ident_bf16[:])
         bias = const.tile([P, 2], F32)
         nc.vector.tensor_copy(out=bias[:], in_=bias_t[:, 0:2])
 
-        centres_t = psum.tile([P, 2, VIEWS, P], BF16, tag="z", bufs=2)
+        centres_t = psum.tile([P, 2, VIEWS, P], BF16, tag="bank")
         for h in range(2):
             for t in range(VIEWS):
                 nc.tensor.transpose(
@@ -116,7 +120,7 @@ def tile_qccpn_pa_t_kernel(
 
         c2_column = const.tile([P, 2], F32)
         c2_repeated = const.tile([P, 2, P], F32)
-        c2_t = psum.tile([P, 2, P], F32, tag="g")
+        c2_t = psum.tile([P, 2, P], F32, tag="bank")
         for h in range(2):
             unread = work.tile([P, VIEWS * FEAT], BF16, tag="unread", bufs=4)
             nc.scalar.activation(
@@ -147,7 +151,7 @@ def tile_qccpn_pa_t_kernel(
             x_rows = x_sb[(u // 2, 2 * (u % 2) + j)]
             grouped[(u, j)] = work.tile([P, SLOTS, P, PACK], BF16, tag="grouped", bufs=4, align_bytes=64, name="grouped")
             for half in range(2):
-                xt = psum.tile([P, 2, 2, P], F32, tag="xt", bufs=4)
+                xt = psum.tile([P, 2, 2, P], F32, tag="bank")
                 for i in range(2):
                     words = x_rows[:, 2 * half + i, :].bitcast(F32)
                     for e in range(2):
@@ -170,7 +174,7 @@ def tile_qccpn_pa_t_kernel(
 
         def project_view(u, j):
             w = weight_of_view[2 * (u % 2) + j]
-            z_bank[(u, j)] = psum.tile([P, CHUNK], F32, tag="z", bufs=2, name="z")
+            z_bank[(u, j)] = psum.tile([P, CHUNK], F32, tag="bank", name="z")
             nc.tensor.matmul_mx(
                 out=z_bank[(u, j)][:],
                 lhsT=w_codes[:, w, :].bitcast(FP8X4),
@@ -195,7 +199,7 @@ def tile_qccpn_pa_t_kernel(
             slot = 2 * (u % 2) + j
             if j == 0:
                 f2[u] = work.tile([P, 2], F32, tag="f2", bufs=4, name="f2")
-            ft = psum.tile([P, VIEWS, FEAT], F32, tag="ft")
+            ft = psum.tile([P, VIEWS, FEAT], F32, tag="bank")
             for v in range(VIEWS):
                 nc.tensor.transpose(
                     out=ft[:, v, :], in_=feat[u // 2][:, v, slot * P : (slot + 1) * P], identity=ident_f32[:]
@@ -220,7 +224,7 @@ def tile_qccpn_pa_t_kernel(
             )
 
         def score(u):
-            g_bank[u] = psum.tile([P, 2, NCLASS], F32, tag="g", name="g")
+            g_bank[u] = psum.tile([P, 2, NCLASS], F32, tag="bank", name="g")
             for j in range(2):
                 nc.tensor.matmul_mx(
                     out=g_bank[u][:, j, :],
@@ -232,11 +236,13 @@ def tile_qccpn_pa_t_kernel(
                     stop=True,
                 )
 
-        def squared_distance(u):
+        def c2_minus_2g(u):
             dist[u] = work.tile([P, 2, NCLASS], F32, tag="dist", bufs=6, name="dist")
             nc.vector.scalar_tensor_tensor(
                 out=dist[u][:], in0=g_bank[u][:], scalar=-2.0, in1=c2_twice[:], op0=ALU.mult, op1=ALU.add
             )
+
+        def add_f2_and_clamp(u):
             for j in range(2):
                 nc.vector.tensor_scalar(
                     out=dist[u][:, j, :],
@@ -258,20 +264,23 @@ def tile_qccpn_pa_t_kernel(
 
         with tc.manual_schedule():
             for step in range(UNITS + AT_STORE):
+                if live(step - AT_DISTANCE):
+                    c2_minus_2g(step - AT_DISTANCE)
                 for j in range(2):
                     if live(step - AT_PROJECT):
                         quantise_view(step - AT_PROJECT, j)
+                if live(step - AT_DISTANCE):
+                    add_f2_and_clamp(step - AT_DISTANCE)
                 if live(step - AT_SCORE):
                     quantise_features(step - AT_SCORE)
-                if live(step - AT_DISTANCE):
-                    squared_distance(step - AT_DISTANCE)
                 for j in range(2):
-                    if live(step - AT_SQUARES):
-                        square_sum(step - AT_SQUARES, j)
                     if live(step - AT_RELU):
                         relu_view(step - AT_RELU, j)
+                for j in range(2):
                     if live(step):
                         transpose_view(step, j)
+                    if live(step - AT_SQUARES):
+                        square_sum(step - AT_SQUARES, j)
                 if live(step - AT_SQUARES):
                     regroup_features(step - AT_SQUARES)
                 for j in range(2):

@@ -35,6 +35,9 @@ AT_SCORE = 5
 AT_DISTANCE = 6
 AT_ROOT = 7
 AT_STORE = 8
+AT_BIASES = AT_RELU - 1
+AT_CENTRES = AT_SCORE - 2
+AT_C2 = AT_DISTANCE - 2
 
 
 def tile_qccpn_pa_t_kernel(
@@ -49,6 +52,7 @@ def tile_qccpn_pa_t_kernel(
         x_pool = ctx.enter_context(tc.tile_pool(name="x", bufs=1))
         work = ctx.enter_context(tc.tile_pool(name="work", bufs=2))
         psum = ctx.enter_context(tc.psum_pool(name="psum", bufs=8))
+        ctx.enter_context(tc.manual_schedule())
 
         ident_f32 = const.tile([P, P], F32)
         masks.make_identity(nc, ident_f32[:])
@@ -84,53 +88,64 @@ def tile_qccpn_pa_t_kernel(
                 in_=words[0].rearrange("p n t -> p (n t)").bitcast(I32),
             )
 
-        nc.scalar.dma_start(out=bias_rows[0:1, :], in_=b_f.rearrange("(o n) -> o n", o=1))
-        nc.scalar.dma_start(out=bias_rows[1:2, :], in_=b_r.rearrange("(o n) -> o n", o=1))
-        nc.sync.dma_start(out=centres_in[:], in_=centers.rearrange("(h c) j -> c h j", c=P))
         load_view(0, 0)
         load_view(0, 1)
-        load_weight(0, W_f_words, W_f_scales)
-        load_weight(1, W_r_words, W_r_scales)
+        nc.sync.dma_start(out=bias_rows[0:1, :], in_=b_f.rearrange("(o n) -> o n", o=1))
+        nc.sync.dma_start(out=bias_rows[1:2, :], in_=b_r.rearrange("(o n) -> o n", o=1))
         load_view(0, 2)
         load_view(0, 3)
-        for c in range(1, CHUNKS):
+        load_weight(0, W_f_words, W_f_scales)
+        load_view(1, 0)
+        load_weight(1, W_r_words, W_r_scales)
+        load_view(1, 1)
+        nc.sync.dma_start(out=centres_in[:], in_=centers.rearrange("(h c) j -> c h j", c=P))
+        load_view(1, 2)
+        load_view(1, 3)
+        for c in range(2, CHUNKS):
             for v in range(VIEWS):
                 load_view(c, v)
 
-        bias_t = psum.tile([P, P], BF16, tag="bank")
-        nc.tensor.transpose(out=bias_t[:], in_=bias_rows[:], identity=ident_bf16[:])
         bias = const.tile([P, 2], F32)
-        nc.vector.tensor_copy(out=bias[:], in_=bias_t[:, 0:2])
-
-        centres_t = psum.tile([P, 2, VIEWS, P], BF16, tag="bank")
-        for h in range(2):
-            for t in range(VIEWS):
-                nc.tensor.transpose(
-                    out=centres_t[:, h, t, :], in_=centres_in[:, h, t * FEAT : (t + 1) * FEAT], identity=ident_bf16[:]
-                )
-        centres_grouped = const.tile([P, 2, P, PACK], BF16, align_bytes=64)
-        nc.vector.tensor_copy(out=centres_grouped[:], in_=centres_t[:].rearrange("p h t c -> p h c t"))
         c_codes = const.tile([P, NCLASS], U32, align_bytes=64)
         c_scales = const.tile([P, NCLASS], U8, align_bytes=64)
-        nc.vector.quantize_mx(
-            out=c_codes[:].bitcast(FP8X4),
-            scales=c_scales[:],
-            in_=centres_grouped[:].rearrange("p h c t -> p (h c t)"),
-        )
-
-        c2_column = const.tile([P, 2], F32)
         c2_repeated = const.tile([P, 2, P], F32)
-        c2_t = psum.tile([P, 2, P], F32, tag="bank")
-        for h in range(2):
-            unread = work.tile([P, VIEWS * FEAT], BF16, tag="unread", bufs=4)
-            nc.scalar.activation(
-                out=unread[:], in_=centres_in[:, h, :], func=ACT.Square, accum_out=c2_column[:, h : h + 1]
-            )
-            nc.vector.tensor_copy(out=c2_repeated[:, h, :], in_=c2_column[:, h : h + 1].to_broadcast([P, P]))
-            nc.tensor.transpose(out=c2_t[:, h, :], in_=c2_repeated[:, h, :], identity=ident_f32[:])
         c2_twice = const.tile([P, 2, NCLASS], F32)
-        for j in range(2):
-            nc.vector.tensor_copy(out=c2_twice[:, j, :], in_=c2_t[:].rearrange("p h c -> p (h c)"))
+
+        def prepare_biases():
+            bias_t = psum.tile([P, P], BF16, tag="bank")
+            nc.tensor.transpose(out=bias_t[:], in_=bias_rows[:], identity=ident_bf16[:])
+            nc.vector.tensor_copy(out=bias[:], in_=bias_t[:, 0:2])
+
+        def prepare_centres():
+            centres_t = psum.tile([P, 2, VIEWS, P], BF16, tag="bank")
+            for h in range(2):
+                for t in range(VIEWS):
+                    nc.tensor.transpose(
+                        out=centres_t[:, h, t, :],
+                        in_=centres_in[:, h, t * FEAT : (t + 1) * FEAT],
+                        identity=ident_bf16[:],
+                    )
+            centres_grouped = const.tile([P, 2, P, PACK], BF16, align_bytes=64)
+            nc.vector.tensor_copy(out=centres_grouped[:], in_=centres_t[:].rearrange("p h t c -> p h c t"))
+            c2_column = const.tile([P, 2], F32)
+            for h in range(2):
+                unread = work.tile([P, VIEWS * FEAT], BF16, tag="unread", bufs=4)
+                nc.scalar.activation(
+                    out=unread[:], in_=centres_in[:, h, :], func=ACT.Square, accum_out=c2_column[:, h : h + 1]
+                )
+                nc.vector.tensor_copy(out=c2_repeated[:, h, :], in_=c2_column[:, h : h + 1].to_broadcast([P, P]))
+            nc.vector.quantize_mx(
+                out=c_codes[:].bitcast(FP8X4),
+                scales=c_scales[:],
+                in_=centres_grouped[:].rearrange("p h c t -> p (h c t)"),
+            )
+
+        def spread_c2():
+            c2_t = psum.tile([P, 2, P], F32, tag="bank")
+            for h in range(2):
+                nc.tensor.transpose(out=c2_t[:, h, :], in_=c2_repeated[:, h, :], identity=ident_f32[:])
+            for j in range(2):
+                nc.vector.tensor_copy(out=c2_twice[:, j, :], in_=c2_t[:].rearrange("p h c -> p (h c)"))
 
         grouped = {}
         x_codes = {}
@@ -158,7 +173,7 @@ def tile_qccpn_pa_t_kernel(
                         nc.tensor.transpose(out=xt[:, i, e, :], in_=words[:, e : IN_F // 2 : 2], identity=ident_f32[:])
                 target = grouped[(u, j)][:, 2 * half : 2 * half + 2, :, :].bitcast(F32)
                 source = xt[:].rearrange("p i e r -> p i r e")
-                if half == 0:
+                if half == 0 or (u % 2 == 0 and j == 0):
                     nc.scalar.copy(out=target, in_=source)
                 else:
                     nc.vector.tensor_copy(out=target, in_=source)
@@ -212,7 +227,10 @@ def tile_qccpn_pa_t_kernel(
         def regroup_features(u):
             columns = slice(2 * (u % 2) * P, (2 * (u % 2) + 2) * P)
             f_grouped[u] = work.tile([P, 2 * P, PACK], BF16, tag="f_grouped", bufs=3, align_bytes=64, name="f_grouped")
-            nc.vector.tensor_copy(out=f_grouped[u][:], in_=feat[u // 2][:, :, columns].rearrange("p v n -> p n v"))
+            nc.vector.tensor_copy(
+                out=f_grouped[u][:].rearrange("p (c i) v -> p c v i", i=4),
+                in_=feat[u // 2][:, :, columns].rearrange("p v (c i) -> p c v i", i=4),
+            )
 
         def quantise_features(u):
             f_codes[u] = work.tile([P, 2 * P], U32, tag="f_codes", bufs=2, align_bytes=64, name="f_codes")
@@ -262,33 +280,38 @@ def tile_qccpn_pa_t_kernel(
             rows = out[c * CHUNK : (c + 1) * CHUNK, :].rearrange("(r s) n -> r s n", s=SLOTS)
             nc.sync.dma_start(out=rows[:, 2 * (u % 2) : 2 * (u % 2) + 2, :], in_=dist[u][:])
 
-        with tc.manual_schedule():
-            for step in range(UNITS + AT_STORE):
-                if live(step - AT_DISTANCE):
-                    c2_minus_2g(step - AT_DISTANCE)
-                for j in range(2):
-                    if live(step - AT_PROJECT):
-                        quantise_view(step - AT_PROJECT, j)
-                if live(step - AT_DISTANCE):
-                    add_f2_and_clamp(step - AT_DISTANCE)
-                if live(step - AT_SCORE):
-                    quantise_features(step - AT_SCORE)
-                for j in range(2):
-                    if live(step - AT_RELU):
-                        relu_view(step - AT_RELU, j)
-                for j in range(2):
-                    if live(step):
-                        transpose_view(step, j)
-                    if live(step - AT_SQUARES):
-                        square_sum(step - AT_SQUARES, j)
+        for step in range(UNITS + AT_STORE):
+            if live(step - AT_DISTANCE):
+                c2_minus_2g(step - AT_DISTANCE)
+            for j in range(2):
+                if live(step - AT_PROJECT):
+                    quantise_view(step - AT_PROJECT, j)
+            if live(step - AT_DISTANCE):
+                add_f2_and_clamp(step - AT_DISTANCE)
+            if live(step - AT_SCORE):
+                quantise_features(step - AT_SCORE)
+            for j in range(2):
+                if live(step - AT_RELU):
+                    relu_view(step - AT_RELU, j)
+            for j in range(2):
+                if live(step):
+                    transpose_view(step, j)
                 if live(step - AT_SQUARES):
-                    regroup_features(step - AT_SQUARES)
-                for j in range(2):
-                    if live(step - AT_PROJECT):
-                        project_view(step - AT_PROJECT, j)
-                if live(step - AT_SCORE):
-                    score(step - AT_SCORE)
-                if live(step - AT_ROOT):
-                    root(step - AT_ROOT)
-                if live(step - AT_STORE):
-                    scale_and_store(step - AT_STORE)
+                    square_sum(step - AT_SQUARES, j)
+            if live(step - AT_SQUARES):
+                regroup_features(step - AT_SQUARES)
+            for j in range(2):
+                if live(step - AT_PROJECT):
+                    project_view(step - AT_PROJECT, j)
+            if live(step - AT_SCORE):
+                score(step - AT_SCORE)
+            if live(step - AT_ROOT):
+                root(step - AT_ROOT)
+            if live(step - AT_STORE):
+                scale_and_store(step - AT_STORE)
+            if step == AT_BIASES:
+                prepare_biases()
+            if step == AT_CENTRES:
+                prepare_centres()
+            if step == AT_C2:
+                spread_c2()

@@ -173,7 +173,7 @@ def tile_qccpn_pa_t_kernel(
                         nc.tensor.transpose(out=xt[:, i, e, :], in_=words[:, e : IN_F // 2 : 2], identity=ident_f32[:])
                 target = grouped[(u, j)][:, 2 * half : 2 * half + 2, :, :].bitcast(F32)
                 source = xt[:].rearrange("p i e r -> p i r e")
-                if half == 0 or (u % 2 == 0 and j == 0):
+                if half == 0:
                     nc.scalar.copy(out=target, in_=source)
                 else:
                     nc.vector.tensor_copy(out=target, in_=source)
@@ -262,7 +262,7 @@ def tile_qccpn_pa_t_kernel(
 
         def add_f2_and_clamp(u):
             for j in range(2):
-                nc.vector.tensor_scalar(
+                nc.gpsimd.tensor_scalar(
                     out=dist[u][:, j, :],
                     in0=dist[u][:, j, :],
                     scalar1=f2[u][:, j : j + 1],
@@ -275,7 +275,9 @@ def tile_qccpn_pa_t_kernel(
             nc.scalar.activation(out=dist[u][:], in_=dist[u][:], func=ACT.Sqrt)
 
         def scale_and_store(u):
-            nc.vector.tensor_scalar(out=dist[u][:], in0=dist[u][:], scalar1=-GAMMA, scalar2=None, op0=ALU.mult)
+            nc.gpsimd.tensor_scalar(
+                out=dist[u][:], in0=dist[u][:], scalar1=-GAMMA, scalar2=0.0, op0=ALU.mult, op1=ALU.add
+            )
             c = u // 2
             rows = out[c * CHUNK : (c + 1) * CHUNK, :].rearrange("(r s) n -> r s n", s=SLOTS)
             nc.sync.dma_start(out=rows[:, 2 * (u % 2) : 2 * (u % 2) + 2, :], in_=dist[u][:])

@@ -33,8 +33,8 @@ AT_RELU = 2
 AT_SQUARES = 4
 AT_SCORE = 5
 AT_DISTANCE = 6
-AT_ROOT = 7
-AT_STORE = 8
+AT_ROOT = 8
+AT_STORE = 9
 AT_BIASES = AT_RELU - 1
 AT_CENTRES = AT_SCORE - 2
 AT_C2 = AT_DISTANCE - 2
@@ -173,7 +173,7 @@ def tile_qccpn_pa_t_kernel(
                         nc.tensor.transpose(out=xt[:, i, e, :], in_=words[:, e : IN_F // 2 : 2], identity=ident_f32[:])
                 target = grouped[(u, j)][:, 2 * half : 2 * half + 2, :, :].bitcast(F32)
                 source = xt[:].rearrange("p i e r -> p i r e")
-                if half == 0:
+                if half == 0 or (u % 2 == 0 and j == 0):
                     nc.scalar.copy(out=target, in_=source)
                 else:
                     nc.vector.tensor_copy(out=target, in_=source)
@@ -262,7 +262,7 @@ def tile_qccpn_pa_t_kernel(
 
         def add_f2_and_clamp(u):
             for j in range(2):
-                nc.gpsimd.tensor_scalar(
+                nc.vector.tensor_scalar(
                     out=dist[u][:, j, :],
                     in0=dist[u][:, j, :],
                     scalar1=f2[u][:, j : j + 1],
@@ -275,42 +275,45 @@ def tile_qccpn_pa_t_kernel(
             nc.scalar.activation(out=dist[u][:], in_=dist[u][:], func=ACT.Sqrt)
 
         def scale_and_store(u):
-            nc.gpsimd.tensor_scalar(
-                out=dist[u][:], in0=dist[u][:], scalar1=-GAMMA, scalar2=0.0, op0=ALU.mult, op1=ALU.add
-            )
+            nc.vector.tensor_scalar(out=dist[u][:], in0=dist[u][:], scalar1=-GAMMA, scalar2=None, op0=ALU.mult)
             c = u // 2
             rows = out[c * CHUNK : (c + 1) * CHUNK, :].rearrange("(r s) n -> r s n", s=SLOTS)
             nc.sync.dma_start(out=rows[:, 2 * (u % 2) : 2 * (u % 2) + 2, :], in_=dist[u][:])
 
         for step in range(UNITS + AT_STORE):
-            if live(step - AT_DISTANCE):
-                c2_minus_2g(step - AT_DISTANCE)
-            for j in range(2):
-                if live(step - AT_PROJECT):
-                    quantise_view(step - AT_PROJECT, j)
-            if live(step - AT_DISTANCE):
-                add_f2_and_clamp(step - AT_DISTANCE)
             if live(step - AT_SCORE):
                 quantise_features(step - AT_SCORE)
+            if live(step - AT_SQUARES):
+                regroup_features(step - AT_SQUARES)
+            if live(step - AT_PROJECT):
+                quantise_view(step - AT_PROJECT, 0)
+            if live(step - AT_DISTANCE):
+                c2_minus_2g(step - AT_DISTANCE)
+            if live(step - AT_PROJECT):
+                quantise_view(step - AT_PROJECT, 1)
             for j in range(2):
                 if live(step - AT_RELU):
                     relu_view(step - AT_RELU, j)
-            for j in range(2):
-                if live(step):
-                    transpose_view(step, j)
-                if live(step - AT_SQUARES):
-                    square_sum(step - AT_SQUARES, j)
+            if live(step):
+                transpose_view(step, 0)
             if live(step - AT_SQUARES):
-                regroup_features(step - AT_SQUARES)
-            for j in range(2):
-                if live(step - AT_PROJECT):
-                    project_view(step - AT_PROJECT, j)
-            if live(step - AT_SCORE):
-                score(step - AT_SCORE)
-            if live(step - AT_ROOT):
-                root(step - AT_ROOT)
+                square_sum(step - AT_SQUARES, 0)
+            if live(step - AT_DISTANCE):
+                add_f2_and_clamp(step - AT_DISTANCE)
             if live(step - AT_STORE):
                 scale_and_store(step - AT_STORE)
+            if live(step):
+                transpose_view(step, 1)
+            if live(step - AT_SQUARES):
+                square_sum(step - AT_SQUARES, 1)
+            if live(step - AT_PROJECT):
+                project_view(step - AT_PROJECT, 0)
+            if live(step - AT_SCORE):
+                score(step - AT_SCORE)
+            if live(step - AT_PROJECT):
+                project_view(step - AT_PROJECT, 1)
+            if live(step - AT_ROOT):
+                root(step - AT_ROOT)
             if step == AT_BIASES:
                 prepare_biases()
             if step == AT_CENTRES:

from contextlib import ExitStack

import concourse.masks as masks
import concourse.mybir as mybir

F32 = mybir.dt.float32
BF16 = mybir.dt.bfloat16
U8 = mybir.dt.uint8
U32 = mybir.dt.uint32
I32 = mybir.dt.int32
FP8X4 = mybir.dt.float8_e4m3fn_x4
ACT = mybir.ActivationFunctionType
ALU = mybir.AluOpType

P = 128
PACK = 4
BATCH = 4096
IN_F = 512
FEAT = 128
VIEWS = 4
NCLASS = 256
GAMMA = 0.1

CHUNK = 512
SLOTS = CHUNK // P
CHUNKS = BATCH // CHUNK
UNITS = 2 * CHUNKS

FLOPS = 2 * BATCH * IN_F * FEAT * VIEWS + 2 * BATCH * FEAT * VIEWS * NCLASS

AT_PROJECT = 1
AT_RELU = 2
AT_SQUARES = 4
AT_SCORE = 5
AT_DISTANCE = 6
AT_ROOT = 8
AT_STORE = 9
AT_BIASES = AT_RELU - 1
AT_CENTRES = AT_SCORE - 2
AT_C2 = AT_DISTANCE - 2


def tile_qccpn_pa_t_kernel(
    tc, x, x_90, x_180, x_270, W_f_words, W_f_scales, b_f, W_r_words, W_r_scales, b_r, centers, out
):
    nc = tc.nc
    views = (x, x_90, x_180, x_270)
    weight_of_view = (0, 1, 1, 1)

    with ExitStack() as ctx:
        const = ctx.enter_context(tc.tile_pool(name="const", bufs=1))
        x_pool = ctx.enter_context(tc.tile_pool(name="x", bufs=1))
        work = ctx.enter_context(tc.tile_pool(name="work", bufs=2))
        psum = ctx.enter_context(tc.psum_pool(name="psum", bufs=8))
        ctx.enter_context(tc.manual_schedule())

        ident_f32 = const.tile([P, P], F32)
        masks.make_identity(nc, ident_f32[:])
        ident_bf16 = const.tile([P, P], BF16)
        masks.make_identity(nc, ident_bf16[:])

        w_codes = const.tile([P, 2, FEAT], U32, align_bytes=64)
        w_scales = const.tile([P, 2, FEAT], U8, align_bytes=64)
        nc.vector.memset(w_scales[:].rearrange("p w n -> p (w n)").bitcast(I32), 0)
        bias_rows = const.tile([P, P], BF16)
        nc.vector.memset(bias_rows[:], 0.0)

        one = const.tile([P, 1], F32)
        nc.vector.memset(one[:], 1.0)
        nc.scalar.activation(out=one[:], in_=one[:], func=ACT.Sqrt)

        centres_in = const.tile([P, 2, VIEWS * FEAT], BF16)
        x_sb = {}

        def load_view(c, v):
            x_sb[(c, v)] = x_pool.tile([P, SLOTS, IN_F], BF16, name="x_%d_%d" % (c, v))
            rows = views[v][c * CHUNK : (c + 1) * CHUNK, :]
            nc.sync.dma_start(out=x_sb[(c, v)][:], in_=rows.rearrange("(r s) k -> r s k", s=SLOTS))

        def load_weight(w, words, scales):
            for quadrant in range(4):
                nc.sync.dma_start(
                    out=w_scales[32 * quadrant : 32 * quadrant + 4, w, :].bitcast(I32),
                    in_=scales[0, 4 * quadrant : 4 * quadrant + 4, :].bitcast(I32),
                )
            nc.sync.dma_start(
                out=w_codes[:, w, :].bitcast(I32),
                in_=words[0].rearrange("p n t -> p (n t)").bitcast(I32),
            )

        load_view(0, 0)
        load_view(0, 1)
        nc.sync.dma_start(out=bias_rows[0:1, :], in_=b_f.rearrange("(o n) -> o n", o=1))
        nc.sync.dma_start(out=bias_rows[1:2, :], in_=b_r.rearrange("(o n) -> o n", o=1))
        load_view(0, 2)
        load_view(0, 3)
        load_weight(0, W_f_words, W_f_scales)
        load_view(1, 0)
        load_weight(1, W_r_words, W_r_scales)
        load_view(1, 1)
        nc.sync.dma_start(out=centres_in[:], in_=centers.rearrange("(h c) j -> c h j", c=P))
        load_view(1, 2)
        load_view(1, 3)
        for c in range(2, CHUNKS):
            for v in range(VIEWS):
                load_view(c, v)

        bias = const.tile([P, 2], F32)
        c_codes = const.tile([P, NCLASS], U32, align_bytes=64)
        c_scales = const.tile([P, NCLASS], U8, align_bytes=64)
        c2_repeated = const.tile([P, 2, P], F32)
        c2_twice = const.tile([P, 2, NCLASS], F32)

        def prepare_biases():
            bias_t = psum.tile([P, P], BF16, tag="bank")
            nc.tensor.transpose(out=bias_t[:], in_=bias_rows[:], identity=ident_bf16[:])
            nc.vector.tensor_copy(out=bias[:], in_=bias_t[:, 0:2])

        def prepare_centres():
            centres_t = psum.tile([P, 2, VIEWS, P], BF16, tag="bank")
            for h in range(2):
                for t in range(VIEWS):
                    nc.tensor.transpose(
                        out=centres_t[:, h, t, :],
                        in_=centres_in[:, h, t * FEAT : (t + 1) * FEAT],
                        identity=ident_bf16[:],
                    )
            centres_grouped = const.tile([P, 2, P, PACK], BF16, align_bytes=64)
            nc.vector.tensor_copy(out=centres_grouped[:], in_=centres_t[:].rearrange("p h t c -> p h c t"))
            c2_column = const.tile([P, 2], F32)
            for h in range(2):
                unread = work.tile([P, VIEWS * FEAT], BF16, tag="unread", bufs=4)
                nc.scalar.activation(
                    out=unread[:], in_=centres_in[:, h, :], func=ACT.Square, accum_out=c2_column[:, h : h + 1]
                )
                nc.vector.tensor_copy(out=c2_repeated[:, h, :], in_=c2_column[:, h : h + 1].to_broadcast([P, P]))
            nc.vector.quantize_mx(
                out=c_codes[:].bitcast(FP8X4),
                scales=c_scales[:],
                in_=centres_grouped[:].rearrange("p h c t -> p (h c t)"),
            )

        def spread_c2():
            c2_t = psum.tile([P, 2, P], F32, tag="bank")
            for h in range(2):
                nc.tensor.transpose(out=c2_t[:, h, :], in_=c2_repeated[:, h, :], identity=ident_f32[:])
            for j in range(2):
                nc.vector.tensor_copy(out=c2_twice[:, j, :], in_=c2_t[:].rearrange("p h c -> p (h c)"))

        grouped = {}
        x_codes = {}
        x_scales = {}
        z_bank = {}
        feat = {}
        f_grouped = {}
        f_codes = {}
        f_scales = {}
        f2 = {}
        g_bank = {}
        dist = {}

        def live(u):
            return 0 <= u < UNITS

        def transpose_view(u, j):
            x_rows = x_sb[(u // 2, 2 * (u % 2) + j)]
            grouped[(u, j)] = work.tile([P, SLOTS, P, PACK], BF16, tag="grouped", bufs=4, align_bytes=64, name="grouped")
            for half in range(2):
                xt = psum.tile([P, 2, 2, P], F32, tag="bank")
                for i in range(2):
                    words = x_rows[:, 2 * half + i, :].bitcast(F32)
                    for e in range(2):
                        nc.tensor.transpose(out=xt[:, i, e, :], in_=words[:, e : IN_F // 2 : 2], identity=ident_f32[:])
                target = grouped[(u, j)][:, 2 * half : 2 * half + 2, :, :].bitcast(F32)
                source = xt[:].rearrange("p i e r -> p i r e")
                if half == 0 or (u % 2 == 0 and j == 0):
                    nc.scalar.copy(out=target, in_=source)
                else:
                    nc.vector.tensor_copy(out=target, in_=source)

        def quantise_view(u, j):
            x_codes[(u, j)] = work.tile([P, CHUNK], U32, tag="x_codes", bufs=4, align_bytes=64, name="x_codes")
            x_scales[(u, j)] = work.tile([P, CHUNK], U8, tag="x_scales", bufs=4, align_bytes=64, name="x_scales")
            nc.vector.quantize_mx(
                out=x_codes[(u, j)][:].bitcast(FP8X4),
                scales=x_scales[(u, j)][:],
                in_=grouped[(u, j)][:].rearrange("p s r t -> p (s r t)"),
            )

        def project_view(u, j):
            w = weight_of_view[2 * (u % 2) + j]
            z_bank[(u, j)] = psum.tile([P, CHUNK], F32, tag="bank", name="z")
            nc.tensor.matmul_mx(
                out=z_bank[(u, j)][:],
                lhsT=w_codes[:, w, :].bitcast(FP8X4),
                lhsT_scale=w_scales[:, w, :],
                rhs=x_codes[(u, j)][:].bitcast(FP8X4),
                rhs_scale=x_scales[(u, j)][:],
                start=True,
                stop=True,
            )

        def relu_view(u, j):
            c = u // 2
            v = 2 * (u % 2) + j
            w = weight_of_view[v]
            if v == 0:
                feat[c] = work.tile([P, VIEWS, CHUNK], F32, tag="feat", bufs=2, name="feat")
            nc.scalar.activation(
                out=feat[c][:, v, :], in_=z_bank[(u, j)][:], func=ACT.Relu, bias=bias[:, w : w + 1], scale=1.0
            )

        def square_sum(u, j):
            slot = 2 * (u % 2) + j
            if j == 0:
                f2[u] = work.tile([P, 2], F32, tag="f2", bufs=4, name="f2")
            ft = psum.tile([P, VIEWS, FEAT], F32, tag="bank")
            for v in range(VIEWS):
                nc.tensor.transpose(
                    out=ft[:, v, :], in_=feat[u // 2][:, v, slot * P : (slot + 1) * P], identity=ident_f32[:]
                )
            unread = work.tile([P, VIEWS * FEAT], BF16, tag="unread", bufs=4)
            nc.scalar.activation(
                out=unread[:], in_=ft[:].rearrange("p v f -> p (v f)"), func=ACT.Square, accum_out=f2[u][:, j : j + 1]
            )

        def regroup_features(u):
            columns = slice(2 * (u % 2) * P, (2 * (u % 2) + 2) * P)
            f_grouped[u] = work.tile([P, 2 * P, PACK], BF16, tag="f_grouped", bufs=3, align_bytes=64, name="f_grouped")
            nc.vector.tensor_copy(
                out=f_grouped[u][:].rearrange("p (c i) v -> p c v i", i=4),
                in_=feat[u // 2][:, :, columns].rearrange("p v (c i) -> p c v i", i=4),
            )

        def quantise_features(u):
            f_codes[u] = work.tile([P, 2 * P], U32, tag="f_codes", bufs=2, align_bytes=64, name="f_codes")
            f_scales[u] = work.tile([P, 2 * P], U8, tag="f_scales", bufs=2, align_bytes=64, name="f_scales")
            nc.vector.quantize_mx(
                out=f_codes[u][:].bitcast(FP8X4),
                scales=f_scales[u][:],
                in_=f_grouped[u][:].rearrange("p n v -> p (n v)"),
            )

        def score(u):
            g_bank[u] = psum.tile([P, 2, NCLASS], F32, tag="bank", name="g")
            for j in range(2):
                nc.tensor.matmul_mx(
                    out=g_bank[u][:, j, :],
                    lhsT=f_codes[u][:, j * P : (j + 1) * P].bitcast(FP8X4),
                    lhsT_scale=f_scales[u][:, j * P : (j + 1) * P],
                    rhs=c_codes[:].bitcast(FP8X4),
                    rhs_scale=c_scales[:],
                    start=True,
                    stop=True,
                )

        def c2_minus_2g(u):
            dist[u] = work.tile([P, 2, NCLASS], F32, tag="dist", bufs=6, name="dist")
            nc.vector.scalar_tensor_tensor(
                out=dist[u][:], in0=g_bank[u][:], scalar=-2.0, in1=c2_twice[:], op0=ALU.mult, op1=ALU.add
            )

        def add_f2_and_clamp(u):
            for j in range(2):
                nc.vector.tensor_scalar(
                    out=dist[u][:, j, :],
                    in0=dist[u][:, j, :],
                    scalar1=f2[u][:, j : j + 1],
                    scalar2=0.0,
                    op0=ALU.add,
                    op1=ALU.max,
                )

        def root(u):
            nc.scalar.activation(out=dist[u][:], in_=dist[u][:], func=ACT.Sqrt)

        def scale_and_store(u):
            nc.vector.tensor_scalar(out=dist[u][:], in0=dist[u][:], scalar1=-GAMMA, scalar2=None, op0=ALU.mult)
            c = u // 2
            rows = out[c * CHUNK : (c + 1) * CHUNK, :].rearrange("(r s) n -> r s n", s=SLOTS)
            nc.sync.dma_start(out=rows[:, 2 * (u % 2) : 2 * (u % 2) + 2, :], in_=dist[u][:])

        for step in range(UNITS + AT_STORE):
            if live(step - AT_SCORE):
                quantise_features(step - AT_SCORE)
            if live(step - AT_SQUARES):
                regroup_features(step - AT_SQUARES)
            if live(step - AT_PROJECT):
                quantise_view(step - AT_PROJECT, 0)
            if live(step - AT_DISTANCE):
                c2_minus_2g(step - AT_DISTANCE)
            if live(step - AT_PROJECT):
                quantise_view(step - AT_PROJECT, 1)
            for j in range(2):
                if live(step - AT_RELU):
                    relu_view(step - AT_RELU, j)
            if live(step):
                transpose_view(step, 0)
            if live(step - AT_SQUARES):
                square_sum(step - AT_SQUARES, 0)
            if live(step - AT_DISTANCE):
                add_f2_and_clamp(step - AT_DISTANCE)
            if live(step - AT_STORE):
                scale_and_store(step - AT_STORE)
            if live(step):
                transpose_view(step, 1)
            if live(step - AT_SQUARES):
                square_sum(step - AT_SQUARES, 1)
            if live(step - AT_PROJECT):
                project_view(step - AT_PROJECT, 0)
            if live(step - AT_SCORE):
                score(step - AT_SCORE)
            if live(step - AT_PROJECT):
                project_view(step - AT_PROJECT, 1)
            if live(step - AT_ROOT):
                root(step - AT_ROOT)
            if step == AT_BIASES:
                prepare_biases()
            if step == AT_CENTRES:
                prepare_centres()
            if step == AT_C2:
                spread_c2()
